import numpy as np
import ml_dtypes


def mxq(x, axis, fmt="e4m3"):
    dtype, down = {"e4m3": (ml_dtypes.float8_e4m3fn, 7), "e5m2": (ml_dtypes.float8_e5m2, 14)}[fmt]
    v = np.moveaxis(np.asarray(x, np.float32).astype(ml_dtypes.bfloat16).astype(np.float64), axis, -1)
    blocks = v.reshape(v.shape[:-1] + (-1, 32))
    amax = np.abs(blocks).max(-1, keepdims=True)
    byte = np.maximum(np.where(amax > 0, np.frexp(amax)[1] - 1 + 127, 0) - down, 1)
    scale = np.exp2(byte - 127.0)
    codes = (blocks / scale).astype(np.float32).astype(dtype).astype(np.float64)
    return np.moveaxis((codes * scale).reshape(v.shape), -1, axis)


WIDE = False


def mx_kscale(k):
    if not WIDE:
        return np.ones(k)
    levels = np.array([10, -10, 5, -5, 0])
    a = np.random.permutation(np.resize(levels, k // 512 * 4)).reshape(k // 512, 4)
    idx = np.arange(k)
    return np.exp2(a[idx // 512, idx % 128 // 32])


BF16 = ml_dtypes.bfloat16


def bf(x):
    return np.asarray(x, np.float32).astype(BF16)


def f64(x):
    return np.asarray(x).astype(np.float64)


E2M1 = np.array([0.0, 0.5, 1.0, 1.5, 2.0, 3.0, 4.0, 6.0, -0.0, -0.5, -1.0, -1.5, -2.0, -3.0, -4.0, -6.0])


def pack_weight(w, fmt):
    k, n = w.shape
    w = f64(bf(w)).reshape(k // 32, 32, n)
    amax = np.abs(w).max(1)
    if fmt == "e4m3":
        byte = np.frexp(amax)[1] - 1 + 127 - 7
    else:
        mant, ex = np.frexp(amax / 6.0)
        byte = np.where(mant > 0.5, ex, ex - 1) + 127
    byte = np.clip(np.where(amax > 0, byte, 1), 1, 254)
    scaled = (w * np.exp2(127.0 - byte)[:, None, :]).reshape(k, n).astype(np.float32)
    by_word = np.ascontiguousarray(scaled.reshape(k // 512, 128, 4, n).transpose(0, 1, 3, 2))
    if fmt == "e4m3":
        words = by_word.astype(ml_dtypes.float8_e4m3fn).view(np.uint8)
    else:
        c = by_word.astype(ml_dtypes.float4_e2m1fn).view(np.uint8) & 0xF
        words = c[..., 0::2] | (c[..., 1::2] << 4)
    return np.ascontiguousarray(words), np.ascontiguousarray(byte.astype(np.uint8).reshape(k // 512, 16, n))


def unpack_weight(words, scales, fmt):
    g, p, n, _ = words.shape
    if fmt == "e4m3":
        vals = np.ascontiguousarray(words).view(ml_dtypes.float8_e4m3fn).astype(np.float64)
    else:
        nib = np.empty((g, p, n, 4), np.uint8)
        nib[..., 0::2] = words & 0xF
        nib[..., 1::2] = words >> 4
        vals = E2M1[nib]
    vals = vals * np.repeat(np.exp2(scales.astype(np.float64) - 127.0), 8, axis=1)[..., None]
    return vals.transpose(0, 1, 3, 2).reshape(g * 512, n)


N, C, H, W, CO, KS, ST = 2, 512, 10, 10, 4096, 3, 1
KK = KS * KS
F = C * KK
RUN = np.lcm(KK, 32)
FMT = "e4m3"


def im2col(x, k, s):
    n, c, h, w = x.shape
    ho = (h - k) // s + 1
    wo = (w - k) // s + 1
    cols = np.stack([x[:, :, i:i + s * (ho - 1) + 1:s, j:j + s * (wo - 1) + 1:s] for i in range(k) for j in range(k)], axis=2)
    cols = cols.transpose(1, 2, 0, 3, 4).reshape(c * k * k, n * ho * wo)
    return cols, (n, ho, wo)


def setup_inputs():
    sc = np.repeat(mx_kscale(F)[::RUN], RUN // KK)
    sf = np.repeat(sc, KK)
    x = bf(np.random.standard_normal((N, C, H, W)) * sc[None, :, None, None])
    weight = np.random.uniform(0.0, 1.0, (CO, F)) * 1.7 / np.sqrt(F) / sf[None, :]
    words, scales = pack_weight(np.ascontiguousarray(weight.T), FMT)
    bias = bf(np.random.uniform(-1.0, 1.0, (CO, 1)) * 0.5)
    return {"x": x, "weight_words": words, "weight_scales": scales, "bias": bias}


def reference(x, weight_words, weight_scales, bias):
    cols, (n, ho, wo) = im2col(f64(x), KS, ST)
    flat = (unpack_weight(weight_words, weight_scales, FMT).T @ mxq(cols, 0, "e4m3")) + f64(bias)
    return flat.reshape(CO, n, ho, wo).transpose(1, 0, 2, 3)

@@ -1,0 +1,193 @@
+from contextlib import ExitStack
+
+import concourse.mybir as mybir
+from concourse.masks import make_identity
+
+F32 = mybir.dt.float32
+BF16 = mybir.dt.bfloat16
+I32 = mybir.dt.int32
+U32 = mybir.dt.uint32
+U8 = mybir.dt.uint8
+FP8X4 = mybir.dt.float8_e4m3fn_x4
+
+P = 128
+GROUPS = 9
+CO = 4096
+BANK = 512
+NBANK = CO // BANK
+G_FULL = 8
+FLOPS = 2 * 4096 * 4608 * 128
+
+
+def tile_sparseconv2d_w_kernel(tc, x, weight_words, weight_scales, bias, out):
+    nc = tc.nc
+    with ExitStack() as ctx:
+        keep = ctx.enter_context(tc.tile_pool(name="keep", bufs=1))
+        work = ctx.enter_context(tc.tile_pool(name="work", bufs=3))
+        psum = ctx.enter_context(tc.psum_pool(name="psum", bufs=1))
+
+        xc = keep.tile([P, 2, 4, 10, 10], BF16, name="xc")
+        nc.sync.dma_start(
+            out=xc[:].rearrange("p n d h w -> p n (d h w)"),
+            in_=x.rearrange("n (p d) h w -> p n (d h w)", d=4),
+        )
+
+        plane_a = keep.tile([P, CO], U8, name="plane_a", align_bytes=64)
+        plane_b = keep.tile([P, CO], U8, name="plane_b", align_bytes=64)
+        plane_c = keep.tile([P, CO // 4], U8, name="plane_c", align_bytes=64)
+        brow = keep.tile([P, BANK], BF16, name="brow")
+        nc.vector.memset(plane_a[:].bitcast(I32), 0)
+        nc.vector.memset(plane_b[:].bitcast(I32), 0)
+        nc.vector.memset(plane_c[:].bitcast(I32), 0)
+        nc.vector.memset(brow[:], 0.0)
+
+        for first, plane in ((0, plane_a), (4, plane_b)):
+            for quad in range(4):
+                nc.sync.dma_start(
+                    out=plane[32 * quad : 32 * quad + 16, :].bitcast(I32),
+                    in_=weight_scales[first : first + 4, 4 * quad : 4 * quad + 4, :].bitcast(I32),
+                )
+        for quad in range(4):
+            nc.sync.dma_start(
+                out=plane_c[32 * quad : 32 * quad + 16, :].bitcast(I32),
+                in_=weight_scales[8, 4 * quad : 4 * quad + 4, :]
+                .rearrange("r (k c) -> k r c", k=4)
+                .bitcast(I32),
+            )
+        nc.sync.dma_start(out=brow[0:NBANK, :], in_=bias.rearrange("(b c) one -> b (c one)", b=NBANK))
+
+        w_full = []
+        for g in range(G_FULL):
+            wg = keep.tile([P, CO], U32, name="w%d" % g, align_bytes=64)
+            nc.sync.dma_start(
+                out=wg[:].bitcast(I32),
+                in_=weight_words[g].rearrange("p n t -> p (n t)").bitcast(I32),
+            )
+            w_full.append(wg)
+        n_tail = GROUPS - G_FULL
+        w_tail = []
+        for b in range(NBANK):
+            wt = keep.tile([P, n_tail, BANK], U32, name="wt%d" % b, align_bytes=64)
+            nc.sync.dma_start(
+                out=wt[:].bitcast(I32),
+                in_=weight_words[G_FULL:GROUPS, :, BANK * b : BANK * (b + 1), :]
+                .rearrange("g p n t -> p g (n t)")
+                .bitcast(I32),
+            )
+            w_tail.append(wt)
+
+        ident = keep.tile([P, P], F32, name="ident")
+        make_identity(nc, ident[:])
+
+        xs = keep.tile([P, 18, P, 2], BF16, name="xs", align_bytes=64)
+        for e in range(36):
+            d, s = divmod(e, 9)
+            i, j = divmod(s, 3)
+            e2, lo = divmod(e, 2)
+            dst = xs[:, e2, :, lo].rearrange("p (n a b) -> p n a b", n=2, a=8)
+            src = xc[:, :, d, i : i + 8, j : j + 8]
+            if e2 % 2 == 0:
+                nc.vector.tensor_copy(out=dst, in_=src)
+            else:
+                nc.scalar.copy(out=dst, in_=src)
+
+        ct = keep.tile([P, 2, P, 9], F32, name="ct")
+        bank_no = 0
+        for u in range(2):
+            for f0, nf in ((0, 4), (4, 4), (8, 1)):
+                t1 = psum.tile([P, 4, P], F32, name="t1_%d_%d" % (u, f0), tag="bank%d" % bank_no)
+                bank_no += 1
+                for a in range(nf):
+                    e2 = 2 * (f0 + a) + u
+                    nc.tensor.transpose(
+                        t1[:, a, :], xs[:, e2].rearrange("p q l -> p (q l)").bitcast(F32), ident[:]
+                    )
+                dst = ct[:, u, :, f0 : f0 + nf]
+                src = t1[:, 0:nf, :].rearrange("q a p -> q p a")
+                if u == 0:
+                    nc.vector.tensor_copy(out=dst, in_=src)
+                else:
+                    nc.scalar.copy(out=dst, in_=src)
+
+        bsort = keep.tile([P, 4, P], F32, name="bsort")
+        nc.vector.tensor_copy(out=bsort[:], in_=brow[:].rearrange("r (j c) -> r c j", c=4))
+        tb = psum.tile([P, 4, P], F32, name="tb", tag="bank6")
+        for c in range(4):
+            nc.tensor.transpose(tb[:, c, :], bsort[:, c, :], ident[:])
+        bias_t = keep.tile([P, NBANK, 4], F32, name="bias_t")
+        nc.vector.tensor_copy(out=bias_t[:], in_=tb[:, :, 0:NBANK].rearrange("j c b -> j b c"))
+
+        cth = ct[:].rearrange("q u p f -> q u (p f)")
+        grouped = keep.tile([P, GROUPS, 4 * P], BF16, name="grouped", align_bytes=64)
+        codes = keep.tile([P, GROUPS, P], U32, name="codes", align_bytes=64)
+        cplane = keep.tile([P, GROUPS, P], U8, name="cplane", align_bytes=64)
+        for m in range(5):
+            g0 = 2 * m
+            ng = min(2, GROUPS - g0)
+            t2 = psum.tile([P, 2, 2, P], F32, name="t2_%d" % m, tag="bank%d" % ((7 + m) % 8))
+            for gl in range(ng):
+                for u in range(2):
+                    nc.tensor.transpose(
+                        t2[:, gl, u, :], cth[:, u, P * (g0 + gl) : P * (g0 + gl + 1)], ident[:]
+                    )
+            dst = grouped[:, g0 : g0 + ng, :].bitcast(F32).rearrange("p g (q u) -> p g q u", u=2)
+            src = t2[:, 0:ng].rearrange("p g u q -> p g q u")
+            if m % 2 == 0:
+                nc.vector.tensor_copy(out=dst, in_=src)
+            else:
+                nc.scalar.copy(out=dst, in_=src)
+            nc.vector.quantize_mx(
+                out=codes[:, g0 : g0 + ng, :].rearrange("p g q -> p (g q)").bitcast(FP8X4),
+                scales=cplane[:, g0 : g0 + ng, :].rearrange("p g q -> p (g q)"),
+                in_=grouped[:, g0 : g0 + ng, :].rearrange("p g c -> p (g c)"),
+            )
+
+        def w_scale(g, b):
+            if g < 4:
+                return plane_a[4 * g : P, BANK * b : BANK * (b + 1)]
+            if g < 8:
+                return plane_b[4 * (g - 4) : P, BANK * b : BANK * (b + 1)]
+            return plane_c[4 * (b // 2) : P, BANK * (b % 2) : BANK * (b % 2 + 1)]
+
+        def mx_pass(acc, g, b):
+            if g < G_FULL:
+                rhs = w_full[g][:, BANK * b : BANK * (b + 1)]
+            else:
+                rhs = w_tail[b][:, g - G_FULL, :]
+            nc.tensor.matmul_mx(
+                out=acc[:],
+                lhsT=codes[:, g, :].bitcast(FP8X4),
+                lhsT_scale=cplane[:, g, :],
+                rhs=rhs.bitcast(FP8X4),
+                rhs_scale=w_scale(g, b),
+                start=(g == 0),
+                stop=(g == GROUPS - 1),
+            )
+
+        accs = []
+        for b in range(NBANK):
+            acc = psum.tile([P, BANK], F32, name="acc%d" % b, tag="bank%d" % b)
+            accs.append(acc)
+        for g in range(G_FULL):
+            for b in range(NBANK):
+                mx_pass(accs[b], g, b)
+
+        for b in range(NBANK):
+            for g in range(G_FULL, GROUPS):
+                mx_pass(accs[b], g, b)
+            s_sb = work.tile([P, 4, P], F32, name="s_sb")
+            nc.scalar.copy(out=s_sb[:], in_=accs[b][:].rearrange("q (j c) -> q c j", c=4))
+            t3 = psum.tile([P, 4, P], F32, name="t3_%d" % b, tag="bank%d" % b)
+            for c in range(4):
+                nc.tensor.transpose(t3[:, c, :], s_sb[:, c, :], ident[:])
+            o_sb = work.tile([P, 2, 4, 64], F32, name="o_sb")
+            nc.vector.tensor_tensor(
+                out=o_sb[:].rearrange("j n c q -> j c n q"),
+                in0=t3[:].rearrange("j c (n q) -> j c n q", n=2),
+                in1=bias_t[:, b, :].unsqueeze(2).unsqueeze(3).to_broadcast([P, 4, 2, 64]),
+                op=mybir.AluOpType.add,
+            )
+            nc.sync.dma_start(
+                out=out[:, BANK * b : BANK * (b + 1)].rearrange("n (j c) p q -> j n (c p q)", c=4),
+                in_=o_sb[:].rearrange("j n c q -> j n (c q)"),
+            )

@@ -23,8 +23,9 @@ def tile_sparseconv2d_w_kernel(tc, x, weight_words, weight_scales, bias, out):
     nc = tc.nc
     with ExitStack() as ctx:
         keep = ctx.enter_context(tc.tile_pool(name="keep", bufs=1))
-        work = ctx.enter_context(tc.tile_pool(name="work", bufs=3))
+        work = ctx.enter_context(tc.tile_pool(name="work", bufs=4))
         psum = ctx.enter_context(tc.psum_pool(name="psum", bufs=1))
+        ctx.enter_context(tc.manual_schedule())
 
         xc = keep.tile([P, 2, 4, 10, 10], BF16, name="xc")
         nc.sync.dma_start(
@@ -109,14 +110,6 @@ def tile_sparseconv2d_w_kernel(tc, x, weight_words, weight_scales, bias, out):
                 else:
                     nc.scalar.copy(out=dst, in_=src)
 
-        bsort = keep.tile([P, 4, P], F32, name="bsort")
-        nc.vector.tensor_copy(out=bsort[:], in_=brow[:].rearrange("r (j c) -> r c j", c=4))
-        tb = psum.tile([P, 4, P], F32, name="tb", tag="bank6")
-        for c in range(4):
-            nc.tensor.transpose(tb[:, c, :], bsort[:, c, :], ident[:])
-        bias_t = keep.tile([P, NBANK, 4], F32, name="bias_t")
-        nc.vector.tensor_copy(out=bias_t[:], in_=tb[:, :, 0:NBANK].rearrange("j c b -> j b c"))
-
         cth = ct[:].rearrange("q u p f -> q u (p f)")
         grouped = keep.tile([P, GROUPS, 4 * P], BF16, name="grouped", align_bytes=64)
         codes = keep.tile([P, GROUPS, P], U32, name="codes", align_bytes=64)
@@ -141,6 +134,14 @@ def tile_sparseconv2d_w_kernel(tc, x, weight_words, weight_scales, bias, out):
                 scales=cplane[:, g0 : g0 + ng, :].rearrange("p g q -> p (g q)"),
                 in_=grouped[:, g0 : g0 + ng, :].rearrange("p g c -> p (g c)"),
             )
+
+        bsort = keep.tile([P, 4, P], F32, name="bsort")
+        nc.vector.tensor_copy(out=bsort[:], in_=brow[:].rearrange("r (j c) -> r c j", c=4))
+        tb = psum.tile([P, 4, P], F32, name="tb", tag="bank6")
+        for c in range(4):
+            nc.tensor.transpose(tb[:, c, :], bsort[:, c, :], ident[:])
+        bias_t = keep.tile([P, NBANK, 4], F32, name="bias_t")
+        nc.vector.tensor_copy(out=bias_t[:], in_=tb[:, :, 0:NBANK].rearrange("j c b -> j b c"))
 
         def w_scale(g, b):
             if g < 4:
@@ -172,14 +173,19 @@ def tile_sparseconv2d_w_kernel(tc, x, weight_words, weight_scales, bias, out):
             for b in range(NBANK):
                 mx_pass(accs[b], g, b)
 
-        for b in range(NBANK):
+        s_tiles = {}
+
+        def close_bank(b):
             for g in range(G_FULL, GROUPS):
                 mx_pass(accs[b], g, b)
             s_sb = work.tile([P, 4, P], F32, name="s_sb")
             nc.scalar.copy(out=s_sb[:], in_=accs[b][:].rearrange("q (j c) -> q c j", c=4))
+            s_tiles[b] = s_sb
+
+        def finish_bank(b):
             t3 = psum.tile([P, 4, P], F32, name="t3_%d" % b, tag="bank%d" % b)
             for c in range(4):
-                nc.tensor.transpose(t3[:, c, :], s_sb[:, c, :], ident[:])
+                nc.tensor.transpose(t3[:, c, :], s_tiles[b][:, c, :], ident[:])
             o_sb = work.tile([P, 2, 4, 64], F32, name="o_sb")
             nc.vector.tensor_tensor(
                 out=o_sb[:].rearrange("j n c q -> j c n q"),
@@ -191,3 +197,16 @@ def tile_sparseconv2d_w_kernel(tc, x, weight_words, weight_scales, bias, out):
                 out=out[:, BANK * b : BANK * (b + 1)].rearrange("n (j c) p q -> j n (c p q)", c=4),
                 in_=o_sb[:].rearrange("j n c q -> j n (c q)"),
             )
+
+        for b in (0, 1, 2, 3):
+            close_bank(b)
+        for b in (0, 1):
+            finish_bank(b)
+        for b in (4, 5):
+            close_bank(b)
+        for b in (2, 3):
+            finish_bank(b)
+        for b in (6, 7):
+            close_bank(b)
+        for b in (4, 5, 6, 7):
+            finish_bank(b)

@@ -37,25 +37,28 @@ def tile_sparseconv2d_w_kernel(tc, x, weight_words, weight_scales, bias, out):
         plane_b = keep.tile([P, CO], U8, name="plane_b", align_bytes=64)
         plane_c = keep.tile([P, CO // 4], U8, name="plane_c", align_bytes=64)
         brow = keep.tile([P, BANK], BF16, name="brow")
+        nc.vector.memset(brow[:], 0.0)
         nc.vector.memset(plane_a[:].bitcast(I32), 0)
         nc.vector.memset(plane_b[:].bitcast(I32), 0)
         nc.vector.memset(plane_c[:].bitcast(I32), 0)
-        nc.vector.memset(brow[:], 0.0)
+        nc.scalar.dma_start(out=brow[0:NBANK, :], in_=bias.rearrange("(b c) one -> b (c one)", b=NBANK))
+
+        ident = keep.tile([P, P], F32, name="ident")
+        make_identity(nc, ident[:])
 
         for first, plane in ((0, plane_a), (4, plane_b)):
             for quad in range(4):
-                nc.sync.dma_start(
-                    out=plane[32 * quad : 32 * quad + 16, :].bitcast(I32),
-                    in_=weight_scales[first : first + 4, 4 * quad : 4 * quad + 4, :].bitcast(I32),
+                nc.gpsimd.dma_start(
+                    out=plane[32 * quad : 32 * quad + 16, :].bitcast(F32),
+                    in_=weight_scales[first : first + 4, 4 * quad : 4 * quad + 4, :].bitcast(F32),
                 )
         for quad in range(4):
-            nc.sync.dma_start(
-                out=plane_c[32 * quad : 32 * quad + 16, :].bitcast(I32),
+            nc.gpsimd.dma_start(
+                out=plane_c[32 * quad : 32 * quad + 16, :].bitcast(F32),
                 in_=weight_scales[8, 4 * quad : 4 * quad + 4, :]
                 .rearrange("r (k c) -> k r c", k=4)
-                .bitcast(I32),
+                .bitcast(F32),
             )
-        nc.sync.dma_start(out=brow[0:NBANK, :], in_=bias.rearrange("(b c) one -> b (c one)", b=NBANK))
 
         w_full = []
         for g in range(G_FULL):
@@ -76,9 +79,6 @@ def tile_sparseconv2d_w_kernel(tc, x, weight_words, weight_scales, bias, out):
                 .bitcast(I32),
             )
             w_tail.append(wt)
-
-        ident = keep.tile([P, P], F32, name="ident")
-        make_identity(nc, ident[:])
 
         xs = keep.tile([P, 18, P, 2], BF16, name="xs", align_bytes=64)
         for e in range(36):

@@ -15,7 +15,7 @@ GROUPS = 9
 CO = 4096
 BANK = 512
 NBANK = CO // BANK
-G_FULL = 8
+G_FULL = 6
 FLOPS = 2 * 4096 * 4608 * 128
 
 
@@ -37,28 +37,25 @@ def tile_sparseconv2d_w_kernel(tc, x, weight_words, weight_scales, bias, out):
         plane_b = keep.tile([P, CO], U8, name="plane_b", align_bytes=64)
         plane_c = keep.tile([P, CO // 4], U8, name="plane_c", align_bytes=64)
         brow = keep.tile([P, BANK], BF16, name="brow")
-        nc.vector.memset(brow[:], 0.0)
         nc.vector.memset(plane_a[:].bitcast(I32), 0)
         nc.vector.memset(plane_b[:].bitcast(I32), 0)
         nc.vector.memset(plane_c[:].bitcast(I32), 0)
-        nc.scalar.dma_start(out=brow[0:NBANK, :], in_=bias.rearrange("(b c) one -> b (c one)", b=NBANK))
-
-        ident = keep.tile([P, P], F32, name="ident")
-        make_identity(nc, ident[:])
+        nc.vector.memset(brow[:], 0.0)
 
         for first, plane in ((0, plane_a), (4, plane_b)):
             for quad in range(4):
-                nc.gpsimd.dma_start(
-                    out=plane[32 * quad : 32 * quad + 16, :].bitcast(F32),
-                    in_=weight_scales[first : first + 4, 4 * quad : 4 * quad + 4, :].bitcast(F32),
+                nc.sync.dma_start(
+                    out=plane[32 * quad : 32 * quad + 16, :].bitcast(I32),
+                    in_=weight_scales[first : first + 4, 4 * quad : 4 * quad + 4, :].bitcast(I32),
                 )
         for quad in range(4):
-            nc.gpsimd.dma_start(
-                out=plane_c[32 * quad : 32 * quad + 16, :].bitcast(F32),
+            nc.sync.dma_start(
+                out=plane_c[32 * quad : 32 * quad + 16, :].bitcast(I32),
                 in_=weight_scales[8, 4 * quad : 4 * quad + 4, :]
                 .rearrange("r (k c) -> k r c", k=4)
-                .bitcast(F32),
+                .bitcast(I32),
             )
+        nc.sync.dma_start(out=brow[0:NBANK, :], in_=bias.rearrange("(b c) one -> b (c one)", b=NBANK))
 
         w_full = []
         for g in range(G_FULL):
@@ -79,6 +76,9 @@ def tile_sparseconv2d_w_kernel(tc, x, weight_words, weight_scales, bias, out):
                 .bitcast(I32),
             )
             w_tail.append(wt)
+
+        ident = keep.tile([P, P], F32, name="ident")
+        make_identity(nc, ident[:])
 
         xs = keep.tile([P, 18, P, 2], BF16, name="xs", align_bytes=64)
         for e in range(36):

@@ -37,10 +37,16 @@ def tile_sparseconv2d_w_kernel(tc, x, weight_words, weight_scales, bias, out):
         plane_b = keep.tile([P, CO], U8, name="plane_b", align_bytes=64)
         plane_c = keep.tile([P, CO // 4], U8, name="plane_c", align_bytes=64)
         brow = keep.tile([P, BANK], BF16, name="brow")
+        nc.vector.memset(brow[:], 0.0)
+        nc.scalar.dma_start(out=brow[0:NBANK, :], in_=bias.rearrange("(b c) one -> b (c one)", b=NBANK))
         nc.vector.memset(plane_a[:].bitcast(I32), 0)
         nc.vector.memset(plane_b[:].bitcast(I32), 0)
         nc.vector.memset(plane_c[:].bitcast(I32), 0)
-        nc.vector.memset(brow[:], 0.0)
+
+        ident = keep.tile([P, P], F32, name="ident")
+        make_identity(nc, ident[:])
+        ident_bf = keep.tile([P, P], BF16, name="ident_bf")
+        make_identity(nc, ident_bf[:])
 
         for first, plane in ((0, plane_a), (4, plane_b)):
             for quad in range(4):
@@ -55,7 +61,6 @@ def tile_sparseconv2d_w_kernel(tc, x, weight_words, weight_scales, bias, out):
                 .rearrange("r (k c) -> k r c", k=4)
                 .bitcast(I32),
             )
-        nc.sync.dma_start(out=brow[0:NBANK, :], in_=bias.rearrange("(b c) one -> b (c one)", b=NBANK))
 
         w_full = []
         for g in range(G_FULL):
@@ -77,40 +82,46 @@ def tile_sparseconv2d_w_kernel(tc, x, weight_words, weight_scales, bias, out):
             )
             w_tail.append(wt)
 
-        ident = keep.tile([P, P], F32, name="ident")
-        make_identity(nc, ident[:])
+        bsort = keep.tile([P, 4, P], F32, name="bsort")
+        nc.scalar.copy(out=bsort[:], in_=brow[:].rearrange("r (j c) -> r c j", c=4))
+        tb = psum.tile([P, 4, P], F32, name="tb", tag="bank6")
+        for c in range(4):
+            nc.tensor.transpose(tb[:, c, :], bsort[:, c, :], ident[:])
+        bias_t = keep.tile([P, NBANK, 4], F32, name="bias_t")
 
-        xs = keep.tile([P, 18, P, 2], BF16, name="xs", align_bytes=64)
-        for e in range(36):
-            d, s = divmod(e, 9)
+        xs = keep.tile([P, 4, 9, P], BF16, name="xs", align_bytes=64)
+        for s in range(9):
             i, j = divmod(s, 3)
-            e2, lo = divmod(e, 2)
-            dst = xs[:, e2, :, lo].rearrange("p (n a b) -> p n a b", n=2, a=8)
-            src = xc[:, :, d, i : i + 8, j : j + 8]
-            if e2 % 2 == 0:
-                nc.vector.tensor_copy(out=dst, in_=src)
+            if s < 7:
+                nc.vector.tensor_copy(
+                    out=xs[:, :, s, :].rearrange("p d (n a b) -> p d n a b", n=2, a=8),
+                    in_=xc[:, :, :, i : i + 8, j : j + 8].rearrange("p n d a b -> p d n a b"),
+                )
             else:
-                nc.scalar.copy(out=dst, in_=src)
-
-        ct = keep.tile([P, 2, P, 9], F32, name="ct")
-        bank_no = 0
-        for u in range(2):
-            for f0, nf in ((0, 4), (4, 4), (8, 1)):
-                t1 = psum.tile([P, 4, P], F32, name="t1_%d_%d" % (u, f0), tag="bank%d" % bank_no)
-                bank_no += 1
-                for a in range(nf):
-                    e2 = 2 * (f0 + a) + u
-                    nc.tensor.transpose(
-                        t1[:, a, :], xs[:, e2].rearrange("p q l -> p (q l)").bitcast(F32), ident[:]
+                for n in range(2):
+                    nc.scalar.copy(
+                        out=xs[:, :, s, 64 * n : 64 * (n + 1)].rearrange("p d (a b) -> p d a b", a=8),
+                        in_=xc[:, n, :, i : i + 8, j : j + 8],
                     )
-                dst = ct[:, u, :, f0 : f0 + nf]
-                src = t1[:, 0:nf, :].rearrange("q a p -> q p a")
+        nc.vector.tensor_copy(out=bias_t[:], in_=tb[:, :, 0:NBANK].rearrange("j c b -> j b c"))
+
+        ct = keep.tile([P, 2, P, 9, 2], BF16, name="ct", align_bytes=64)
+        bank_no = 0
+        for f0, nf in ((0, 4), (4, 4), (8, 1)):
+            for u in range(2):
+                t1 = psum.tile([P, 8, P], BF16, name="t1_%d_%d" % (u, f0), tag="bank%d" % bank_no)
+                bank_no += 1
+                for a in range(2 * nf):
+                    e = 4 * (f0 + a // 2) + 2 * u + a % 2
+                    nc.tensor.transpose(t1[:, a, :], xs[:, e // 9, e % 9, :], ident_bf[:])
+                dst = ct[:, u, :, f0 : f0 + nf, :].rearrange("q p f l -> q p (f l)")
+                src = t1[:, 0 : 2 * nf, :].rearrange("q a p -> q p a")
                 if u == 0:
                     nc.vector.tensor_copy(out=dst, in_=src)
                 else:
                     nc.scalar.copy(out=dst, in_=src)
 
-        cth = ct[:].rearrange("q u p f -> q u (p f)")
+        cth = ct[:].rearrange("q u p f l -> q u (p f l)").bitcast(F32)
         grouped = keep.tile([P, GROUPS, 4 * P], BF16, name="grouped", align_bytes=64)
         codes = keep.tile([P, GROUPS, P], U32, name="codes", align_bytes=64)
         cplane = keep.tile([P, GROUPS, P], U8, name="cplane", align_bytes=64)
@@ -134,14 +145,6 @@ def tile_sparseconv2d_w_kernel(tc, x, weight_words, weight_scales, bias, out):
                 scales=cplane[:, g0 : g0 + ng, :].rearrange("p g q -> p (g q)"),
                 in_=grouped[:, g0 : g0 + ng, :].rearrange("p g c -> p (g c)"),
             )
-
-        bsort = keep.tile([P, 4, P], F32, name="bsort")
-        nc.vector.tensor_copy(out=bsort[:], in_=brow[:].rearrange("r (j c) -> r c j", c=4))
-        tb = psum.tile([P, 4, P], F32, name="tb", tag="bank6")
-        for c in range(4):
-            nc.tensor.transpose(tb[:, c, :], bsort[:, c, :], ident[:])
-        bias_t = keep.tile([P, NBANK, 4], F32, name="bias_t")
-        nc.vector.tensor_copy(out=bias_t[:], in_=tb[:, :, 0:NBANK].rearrange("j c b -> j b c"))
 
         def w_scale(g, b):
             if g < 4:

@@ -23,7 +23,7 @@ def tile_sparseconv2d_w_kernel(tc, x, weight_words, weight_scales, bias, out):
     nc = tc.nc
     with ExitStack() as ctx:
         keep = ctx.enter_context(tc.tile_pool(name="keep", bufs=1))
-        work = ctx.enter_context(tc.tile_pool(name="work", bufs=4))
+        work = ctx.enter_context(tc.tile_pool(name="work", bufs=NBANK))
         psum = ctx.enter_context(tc.psum_pool(name="psum", bufs=1))
         ctx.enter_context(tc.manual_schedule())
 
@@ -70,17 +70,30 @@ def tile_sparseconv2d_w_kernel(tc, x, weight_words, weight_scales, bias, out):
                 in_=weight_words[g].rearrange("p n t -> p (n t)").bitcast(I32),
             )
             w_full.append(wg)
-        n_tail = GROUPS - G_FULL
-        w_tail = []
-        for b in range(NBANK):
-            wt = keep.tile([P, n_tail, BANK], U32, name="wt%d" % b, align_bytes=64)
+        w_at = {}
+
+        def load_tail(name, first_group, n_groups, first_bank, n_banks):
+            cols = BANK * n_banks
+            wt = keep.tile([P, n_groups, cols], U32, name=name, align_bytes=64)
             nc.sync.dma_start(
                 out=wt[:].bitcast(I32),
-                in_=weight_words[G_FULL:GROUPS, :, BANK * b : BANK * (b + 1), :]
+                in_=weight_words[
+                    first_group : first_group + n_groups, :, BANK * first_bank : BANK * first_bank + cols, :
+                ]
                 .rearrange("g p n t -> p g (n t)")
                 .bitcast(I32),
             )
-            w_tail.append(wt)
+            for g in range(n_groups):
+                for b in range(n_banks):
+                    w_at[first_group + g, first_bank + b] = (wt, g, BANK * b)
+
+        load_tail("wt01", 6, 3, 0, 2)
+        load_tail("wt23", 6, 3, 2, 2)
+        load_tail("wt6h", 6, 1, 4, 4)
+        load_tail("wt7h", 7, 1, 4, 4)
+        load_tail("wt8_45", 8, 1, 4, 2)
+        load_tail("wt8_6", 8, 1, 6, 1)
+        load_tail("wt8_7", 8, 1, 7, 1)
 
         bsort = keep.tile([P, 4, P], F32, name="bsort")
         nc.scalar.copy(out=bsort[:], in_=brow[:].rearrange("r (j c) -> r c j", c=4))
@@ -157,7 +170,8 @@ def tile_sparseconv2d_w_kernel(tc, x, weight_words, weight_scales, bias, out):
             if g < G_FULL:
                 rhs = w_full[g][:, BANK * b : BANK * (b + 1)]
             else:
-                rhs = w_tail[b][:, g - G_FULL, :]
+                wt, gi, c0 = w_at[g, b]
+                rhs = wt[:, gi, c0 : c0 + BANK]
             nc.tensor.matmul_mx(
                 out=acc[:],
                 lhsT=codes[:, g, :].bitcast(FP8X4),
@@ -178,9 +192,7 @@ def tile_sparseconv2d_w_kernel(tc, x, weight_words, weight_scales, bias, out):
 
         s_tiles = {}
 
-        def close_bank(b):
-            for g in range(G_FULL, GROUPS):
-                mx_pass(accs[b], g, b)
+        def drain_bank(b):
             s_sb = work.tile([P, 4, P], F32, name="s_sb")
             nc.scalar.copy(out=s_sb[:], in_=accs[b][:].rearrange("q (j c) -> q c j", c=4))
             s_tiles[b] = s_sb
@@ -201,15 +213,21 @@ def tile_sparseconv2d_w_kernel(tc, x, weight_words, weight_scales, bias, out):
                 in_=o_sb[:].rearrange("j n c q -> j n (c q)"),
             )
 
-        for b in (0, 1, 2, 3):
-            close_bank(b)
-        for b in (0, 1):
-            finish_bank(b)
-        for b in (4, 5):
-            close_bank(b)
-        for b in (2, 3):
-            finish_bank(b)
-        for b in (6, 7):
-            close_bank(b)
-        for b in (4, 5, 6, 7):
+        for pair in ((0, 1), (2, 3)):
+            for b in pair:
+                for g in range(G_FULL, GROUPS):
+                    mx_pass(accs[b], g, b)
+                drain_bank(b)
+            for b in pair:
+                finish_bank(b)
+        for g in (6, 7):
+            for b in (4, 5, 6, 7):
+                mx_pass(accs[b], g, b)
+        for b in (4, 5, 6):
+            mx_pass(accs[b], 8, b)
+            drain_bank(b)
+        finish_bank(4)
+        mx_pass(accs[7], 8, 7)
+        drain_bank(7)
+        for b in (5, 6, 7):
             finish_bank(b)

@@ -15,7 +15,7 @@ GROUPS = 9
 CO = 4096
 BANK = 512
 NBANK = CO // BANK
-G_FULL = 6
+G_FULL = 4
 FLOPS = 2 * 4096 * 4608 * 128
 
 
@@ -48,12 +48,32 @@ def tile_sparseconv2d_w_kernel(tc, x, weight_words, weight_scales, bias, out):
         ident_bf = keep.tile([P, P], BF16, name="ident_bf")
         make_identity(nc, ident_bf[:])
 
-        for first, plane in ((0, plane_a), (4, plane_b)):
+        w_at = {}
+
+        def load_words(g, first_bank, n_banks):
+            cols = BANK * n_banks
+            wt = keep.tile([P, cols], U32, name="w%d_%d" % (g, first_bank), align_bytes=64)
+            nc.sync.dma_start(
+                out=wt[:].bitcast(I32),
+                in_=weight_words[g, :, BANK * first_bank : BANK * first_bank + cols, :]
+                .rearrange("p n t -> p (n t)")
+                .bitcast(I32),
+            )
+            for b in range(n_banks):
+                w_at[g, first_bank + b] = (wt, BANK * b)
+
+        def load_scales(plane, first):
             for quad in range(4):
                 nc.sync.dma_start(
                     out=plane[32 * quad : 32 * quad + 16, :].bitcast(I32),
                     in_=weight_scales[first : first + 4, 4 * quad : 4 * quad + 4, :].bitcast(I32),
                 )
+
+        load_words(0, 0, NBANK)
+        load_scales(plane_a, 0)
+        load_words(1, 0, NBANK)
+        load_scales(plane_b, 4)
+        load_words(2, 0, NBANK)
         for quad in range(4):
             nc.sync.dma_start(
                 out=plane_c[32 * quad : 32 * quad + 16, :].bitcast(I32),
@@ -61,39 +81,14 @@ def tile_sparseconv2d_w_kernel(tc, x, weight_words, weight_scales, bias, out):
                 .rearrange("r (k c) -> k r c", k=4)
                 .bitcast(I32),
             )
-
-        w_full = []
-        for g in range(G_FULL):
-            wg = keep.tile([P, CO], U32, name="w%d" % g, align_bytes=64)
-            nc.sync.dma_start(
-                out=wg[:].bitcast(I32),
-                in_=weight_words[g].rearrange("p n t -> p (n t)").bitcast(I32),
-            )
-            w_full.append(wg)
-        w_at = {}
-
-        def load_tail(name, first_group, n_groups, first_bank, n_banks):
-            cols = BANK * n_banks
-            wt = keep.tile([P, n_groups, cols], U32, name=name, align_bytes=64)
-            nc.sync.dma_start(
-                out=wt[:].bitcast(I32),
-                in_=weight_words[
-                    first_group : first_group + n_groups, :, BANK * first_bank : BANK * first_bank + cols, :
-                ]
-                .rearrange("g p n t -> p g (n t)")
-                .bitcast(I32),
-            )
-            for g in range(n_groups):
-                for b in range(n_banks):
-                    w_at[first_group + g, first_bank + b] = (wt, g, BANK * b)
-
-        load_tail("wt01", 6, 3, 0, 2)
-        load_tail("wt23", 6, 3, 2, 2)
-        load_tail("wt6h", 6, 1, 4, 4)
-        load_tail("wt7h", 7, 1, 4, 4)
-        load_tail("wt8_45", 8, 1, 4, 2)
-        load_tail("wt8_6", 8, 1, 6, 1)
-        load_tail("wt8_7", 8, 1, 7, 1)
+        load_words(3, 0, NBANK)
+        for first_bank, n_banks in ((0, 4), (4, 2)):
+            for g in range(G_FULL, GROUPS):
+                load_words(g, first_bank, n_banks)
+        for g in range(G_FULL, GROUPS - 1):
+            load_words(g, 6, 2)
+        load_words(8, 6, 1)
+        load_words(8, 7, 1)
 
         bsort = keep.tile([P, 4, P], F32, name="bsort")
         nc.scalar.copy(out=bsort[:], in_=brow[:].rearrange("r (j c) -> r c j", c=4))
@@ -167,11 +162,8 @@ def tile_sparseconv2d_w_kernel(tc, x, weight_words, weight_scales, bias, out):
             return plane_c[4 * (b // 2) : P, BANK * (b % 2) : BANK * (b % 2 + 1)]
 
         def mx_pass(acc, g, b):
-            if g < G_FULL:
-                rhs = w_full[g][:, BANK * b : BANK * (b + 1)]
-            else:
-                wt, gi, c0 = w_at[g, b]
-                rhs = wt[:, gi, c0 : c0 + BANK]
+            wt, c0 = w_at[g, b]
+            rhs = wt[:, c0 : c0 + BANK]
             nc.tensor.matmul_mx(
                 out=acc[:],
                 lhsT=codes[:, g, :].bitcast(FP8X4),
@@ -213,21 +205,26 @@ def tile_sparseconv2d_w_kernel(tc, x, weight_words, weight_scales, bias, out):
                 in_=o_sb[:].rearrange("j n c q -> j n (c q)"),
             )
 
-        for pair in ((0, 1), (2, 3)):
-            for b in pair:
-                for g in range(G_FULL, GROUPS):
-                    mx_pass(accs[b], g, b)
-                drain_bank(b)
-            for b in pair:
-                finish_bank(b)
-        for g in (6, 7):
-            for b in (4, 5, 6, 7):
+        def passes(g, banks):
+            for b in banks:
                 mx_pass(accs[b], g, b)
-        for b in (4, 5, 6):
-            mx_pass(accs[b], 8, b)
-            drain_bank(b)
+                if g == GROUPS - 1:
+                    drain_bank(b)
+
+        for g in range(G_FULL, GROUPS):
+            passes(g, (0, 1, 2, 3))
+        passes(4, (4, 5))
+        finish_bank(0)
+        finish_bank(1)
+        passes(5, (4, 5))
+        finish_bank(2)
+        finish_bank(3)
+        for g in (6, 7, 8):
+            passes(g, (4, 5))
+        passes(4, (6, 7))
         finish_bank(4)
-        mx_pass(accs[7], 8, 7)
-        drain_bank(7)
-        for b in (5, 6, 7):
-            finish_bank(b)
+        finish_bank(5)
+        for g in (5, 6, 7, 8):
+            passes(g, (6, 7))
+        finish_bank(6)
+        finish_bank(7)

@@ -69,11 +69,8 @@ def tile_sparseconv2d_w_kernel(tc, x, weight_words, weight_scales, bias, out):
                     in_=weight_scales[first : first + 4, 4 * quad : 4 * quad + 4, :].bitcast(I32),
                 )
 
-        load_words(0, 0, NBANK)
         load_scales(plane_a, 0)
-        load_words(1, 0, NBANK)
         load_scales(plane_b, 4)
-        load_words(2, 0, NBANK)
         for quad in range(4):
             nc.sync.dma_start(
                 out=plane_c[32 * quad : 32 * quad + 16, :].bitcast(I32),
@@ -81,7 +78,8 @@ def tile_sparseconv2d_w_kernel(tc, x, weight_words, weight_scales, bias, out):
                 .rearrange("r (k c) -> k r c", k=4)
                 .bitcast(I32),
             )
-        load_words(3, 0, NBANK)
+        for g in range(G_FULL):
+            load_words(g, 0, NBANK)
         for first_bank, n_banks in ((0, 4), (4, 2)):
             for g in range(G_FULL, GROUPS):
                 load_words(g, first_bank, n_banks)

@@ -36,17 +36,17 @@ def tile_sparseconv2d_w_kernel(tc, x, weight_words, weight_scales, bias, out):
         plane_a = keep.tile([P, CO], U8, name="plane_a", align_bytes=64)
         plane_b = keep.tile([P, CO], U8, name="plane_b", align_bytes=64)
         plane_c = keep.tile([P, CO // 4], U8, name="plane_c", align_bytes=64)
-        brow = keep.tile([P, BANK], BF16, name="brow")
-        nc.vector.memset(brow[:], 0.0)
-        nc.scalar.dma_start(out=brow[0:NBANK, :], in_=bias.rearrange("(b c) one -> b (c one)", b=NBANK))
         nc.vector.memset(plane_a[:].bitcast(I32), 0)
         nc.vector.memset(plane_b[:].bitcast(I32), 0)
         nc.vector.memset(plane_c[:].bitcast(I32), 0)
+        brow = keep.tile([P, BANK], BF16, name="brow")
+        nc.gpsimd.memset(brow[:], 0.0)
+        nc.scalar.dma_start(out=brow[0:NBANK, :], in_=bias.rearrange("(b c) one -> b (c one)", b=NBANK))
 
-        ident = keep.tile([P, P], F32, name="ident")
-        make_identity(nc, ident[:])
         ident_bf = keep.tile([P, P], BF16, name="ident_bf")
         make_identity(nc, ident_bf[:])
+        ident = keep.tile([P, P], F32, name="ident")
+        make_identity(nc, ident[:])
 
         w_at = {}
 
@@ -64,19 +64,19 @@ def tile_sparseconv2d_w_kernel(tc, x, weight_words, weight_scales, bias, out):
 
         def load_scales(plane, first):
             for quad in range(4):
-                nc.sync.dma_start(
-                    out=plane[32 * quad : 32 * quad + 16, :].bitcast(I32),
-                    in_=weight_scales[first : first + 4, 4 * quad : 4 * quad + 4, :].bitcast(I32),
+                nc.gpsimd.dma_start(
+                    out=plane[32 * quad : 32 * quad + 16, :].bitcast(F32),
+                    in_=weight_scales[first : first + 4, 4 * quad : 4 * quad + 4, :].bitcast(F32),
                 )
 
         load_scales(plane_a, 0)
         load_scales(plane_b, 4)
         for quad in range(4):
-            nc.sync.dma_start(
-                out=plane_c[32 * quad : 32 * quad + 16, :].bitcast(I32),
+            nc.gpsimd.dma_start(
+                out=plane_c[32 * quad : 32 * quad + 16, :].bitcast(F32),
                 in_=weight_scales[8, 4 * quad : 4 * quad + 4, :]
                 .rearrange("r (k c) -> k r c", k=4)
-                .bitcast(I32),
+                .bitcast(F32),
             )
         for g in range(G_FULL):
             load_words(g, 0, NBANK)
@@ -87,13 +87,6 @@ def tile_sparseconv2d_w_kernel(tc, x, weight_words, weight_scales, bias, out):
             load_words(g, 6, 2)
         load_words(8, 6, 1)
         load_words(8, 7, 1)
-
-        bsort = keep.tile([P, 4, P], F32, name="bsort")
-        nc.scalar.copy(out=bsort[:], in_=brow[:].rearrange("r (j c) -> r c j", c=4))
-        tb = psum.tile([P, 4, P], F32, name="tb", tag="bank6")
-        for c in range(4):
-            nc.tensor.transpose(tb[:, c, :], bsort[:, c, :], ident[:])
-        bias_t = keep.tile([P, NBANK, 4], F32, name="bias_t")
 
         xs = keep.tile([P, 4, 9, P], BF16, name="xs", align_bytes=64)
         for s in range(9):
@@ -109,7 +102,6 @@ def tile_sparseconv2d_w_kernel(tc, x, weight_words, weight_scales, bias, out):
                         out=xs[:, :, s, 64 * n : 64 * (n + 1)].rearrange("p d (a b) -> p d a b", a=8),
                         in_=xc[:, n, :, i : i + 8, j : j + 8],
                     )
-        nc.vector.tensor_copy(out=bias_t[:], in_=tb[:, :, 0:NBANK].rearrange("j c b -> j b c"))
 
         ct = keep.tile([P, 2, P, 9, 2], BF16, name="ct", align_bytes=64)
         bank_no = 0
@@ -151,6 +143,14 @@ def tile_sparseconv2d_w_kernel(tc, x, weight_words, weight_scales, bias, out):
                 scales=cplane[:, g0 : g0 + ng, :].rearrange("p g q -> p (g q)"),
                 in_=grouped[:, g0 : g0 + ng, :].rearrange("p g c -> p (g c)"),
             )
+
+        bsort = keep.tile([P, 4, P], F32, name="bsort")
+        nc.scalar.copy(out=bsort[:], in_=brow[:].rearrange("r (j c) -> r c j", c=4))
+        tb = psum.tile([P, 4, P], F32, name="tb", tag="bank4")
+        for c in range(4):
+            nc.tensor.transpose(tb[:, c, :], bsort[:, c, :], ident[:])
+        bias_t = keep.tile([P, NBANK, 4], F32, name="bias_t")
+        nc.vector.tensor_copy(out=bias_t[:], in_=tb[:, :, 0:NBANK].rearrange("j c b -> j b c"))
 
         def w_scale(g, b):
             if g < 4:

@@ -27,32 +27,32 @@ def tile_sparseconv2d_w_kernel(tc, x, weight_words, weight_scales, bias, out):
         psum = ctx.enter_context(tc.psum_pool(name="psum", bufs=1))
         ctx.enter_context(tc.manual_schedule())
 
-        xc = keep.tile([P, 2, 4, 10, 10], BF16, name="xc")
+        xc = keep.tile([P, 2, 4, 10, 10], BF16, name="xc", align_bytes=256)
         nc.sync.dma_start(
             out=xc[:].rearrange("p n d h w -> p n (d h w)"),
             in_=x.rearrange("n (p d) h w -> p n (d h w)", d=4),
         )
 
-        plane_a = keep.tile([P, CO], U8, name="plane_a", align_bytes=64)
-        plane_b = keep.tile([P, CO], U8, name="plane_b", align_bytes=64)
-        plane_c = keep.tile([P, CO // 4], U8, name="plane_c", align_bytes=64)
+        plane_a = keep.tile([P, CO], U8, name="plane_a", align_bytes=256)
+        plane_b = keep.tile([P, CO], U8, name="plane_b", align_bytes=256)
+        plane_c = keep.tile([P, CO // 4], U8, name="plane_c", align_bytes=256)
         nc.vector.memset(plane_a[:].bitcast(I32), 0)
         nc.vector.memset(plane_b[:].bitcast(I32), 0)
         nc.vector.memset(plane_c[:].bitcast(I32), 0)
-        brow = keep.tile([P, BANK], BF16, name="brow")
+        brow = keep.tile([P, BANK], BF16, name="brow", align_bytes=256)
         nc.gpsimd.memset(brow[:], 0.0)
         nc.scalar.dma_start(out=brow[0:NBANK, :], in_=bias.rearrange("(b c) one -> b (c one)", b=NBANK))
 
-        ident_bf = keep.tile([P, P], BF16, name="ident_bf")
+        ident_bf = keep.tile([P, P], BF16, name="ident_bf", align_bytes=256)
         make_identity(nc, ident_bf[:])
-        ident = keep.tile([P, P], F32, name="ident")
+        ident = keep.tile([P, P], F32, name="ident", align_bytes=256)
         make_identity(nc, ident[:])
 
         w_at = {}
 
         def load_words(g, first_bank, n_banks):
             cols = BANK * n_banks
-            wt = keep.tile([P, cols], U32, name="w%d_%d" % (g, first_bank), align_bytes=64)
+            wt = keep.tile([P, cols], U32, name="w%d_%d" % (g, first_bank), align_bytes=256)
             nc.sync.dma_start(
                 out=wt[:].bitcast(I32),
                 in_=weight_words[g, :, BANK * first_bank : BANK * first_bank + cols, :]
@@ -88,7 +88,7 @@ def tile_sparseconv2d_w_kernel(tc, x, weight_words, weight_scales, bias, out):
         load_words(8, 6, 1)
         load_words(8, 7, 1)
 
-        xs = keep.tile([P, 4, 9, P], BF16, name="xs", align_bytes=64)
+        xs = keep.tile([P, 4, 9, P], BF16, name="xs", align_bytes=256)
         for s in range(9):
             i, j = divmod(s, 3)
             if s < 7:
@@ -103,7 +103,7 @@ def tile_sparseconv2d_w_kernel(tc, x, weight_words, weight_scales, bias, out):
                         in_=xc[:, n, :, i : i + 8, j : j + 8],
                     )
 
-        ct = keep.tile([P, 2, P, 9, 2], BF16, name="ct", align_bytes=64)
+        ct = keep.tile([P, 2, P, 9, 2], BF16, name="ct", align_bytes=256)
         bank_no = 0
         for f0, nf in ((0, 4), (4, 4), (8, 1)):
             for u in range(2):
@@ -120,9 +120,9 @@ def tile_sparseconv2d_w_kernel(tc, x, weight_words, weight_scales, bias, out):
                     nc.scalar.copy(out=dst, in_=src)
 
         cth = ct[:].rearrange("q u p f l -> q u (p f l)").bitcast(F32)
-        grouped = keep.tile([P, GROUPS, 4 * P], BF16, name="grouped", align_bytes=64)
-        codes = keep.tile([P, GROUPS, P], U32, name="codes", align_bytes=64)
-        cplane = keep.tile([P, GROUPS, P], U8, name="cplane", align_bytes=64)
+        grouped = keep.tile([P, GROUPS, 4 * P], BF16, name="grouped", align_bytes=256)
+        codes = keep.tile([P, GROUPS, P], U32, name="codes", align_bytes=256)
+        cplane = keep.tile([P, GROUPS, P], U8, name="cplane", align_bytes=256)
         for m in range(5):
             g0 = 2 * m
             ng = min(2, GROUPS - g0)
@@ -144,12 +144,12 @@ def tile_sparseconv2d_w_kernel(tc, x, weight_words, weight_scales, bias, out):
                 in_=grouped[:, g0 : g0 + ng, :].rearrange("p g c -> p (g c)"),
             )
 
-        bsort = keep.tile([P, 4, P], F32, name="bsort")
+        bsort = keep.tile([P, 4, P], F32, name="bsort", align_bytes=256)
         nc.scalar.copy(out=bsort[:], in_=brow[:].rearrange("r (j c) -> r c j", c=4))
         tb = psum.tile([P, 4, P], F32, name="tb", tag="bank4")
         for c in range(4):
             nc.tensor.transpose(tb[:, c, :], bsort[:, c, :], ident[:])
-        bias_t = keep.tile([P, NBANK, 4], F32, name="bias_t")
+        bias_t = keep.tile([P, NBANK, 4], F32, name="bias_t", align_bytes=256)
         nc.vector.tensor_copy(out=bias_t[:], in_=tb[:, :, 0:NBANK].rearrange("j c b -> j b c"))
 
         def w_scale(g, b):
@@ -183,7 +183,7 @@ def tile_sparseconv2d_w_kernel(tc, x, weight_words, weight_scales, bias, out):
         s_tiles = {}
 
         def drain_bank(b):
-            s_sb = work.tile([P, 4, P], F32, name="s_sb")
+            s_sb = work.tile([P, 4, P], F32, name="s_sb", align_bytes=256)
             nc.scalar.copy(out=s_sb[:], in_=accs[b][:].rearrange("q (j c) -> q c j", c=4))
             s_tiles[b] = s_sb
 
@@ -191,7 +191,7 @@ def tile_sparseconv2d_w_kernel(tc, x, weight_words, weight_scales, bias, out):
             t3 = psum.tile([P, 4, P], F32, name="t3_%d" % b, tag="bank%d" % b)
             for c in range(4):
                 nc.tensor.transpose(t3[:, c, :], s_tiles[b][:, c, :], ident[:])
-            o_sb = work.tile([P, 2, 4, 64], F32, name="o_sb")
+            o_sb = work.tile([P, 2, 4, 64], F32, name="o_sb", align_bytes=256)
             nc.vector.tensor_tensor(
                 out=o_sb[:].rearrange("j n c q -> j c n q"),
                 in0=t3[:].rearrange("j c (n q) -> j c n q", n=2),

from contextlib import ExitStack

import concourse.mybir as mybir
from concourse.masks import make_identity

F32 = mybir.dt.float32
BF16 = mybir.dt.bfloat16
I32 = mybir.dt.int32
U32 = mybir.dt.uint32
U8 = mybir.dt.uint8
FP8X4 = mybir.dt.float8_e4m3fn_x4

P = 128
GROUPS = 9
CO = 4096
BANK = 512
NBANK = CO // BANK
G_FULL = 4
FLOPS = 2 * 4096 * 4608 * 128


def tile_sparseconv2d_w_kernel(tc, x, weight_words, weight_scales, bias, out):
    nc = tc.nc
    with ExitStack() as ctx:
        keep = ctx.enter_context(tc.tile_pool(name="keep", bufs=1))
        work = ctx.enter_context(tc.tile_pool(name="work", bufs=NBANK))
        psum = ctx.enter_context(tc.psum_pool(name="psum", bufs=1))
        ctx.enter_context(tc.manual_schedule())

        xc = keep.tile([P, 2, 4, 10, 10], BF16, name="xc", align_bytes=256)
        nc.sync.dma_start(
            out=xc[:].rearrange("p n d h w -> p n (d h w)"),
            in_=x.rearrange("n (p d) h w -> p n (d h w)", d=4),
        )

        plane_a = keep.tile([P, CO], U8, name="plane_a", align_bytes=256)
        plane_b = keep.tile([P, CO], U8, name="plane_b", align_bytes=256)
        plane_c = keep.tile([P, CO // 4], U8, name="plane_c", align_bytes=256)
        nc.vector.memset(plane_a[:].bitcast(I32), 0)
        nc.vector.memset(plane_b[:].bitcast(I32), 0)
        nc.vector.memset(plane_c[:].bitcast(I32), 0)
        brow = keep.tile([P, BANK], BF16, name="brow", align_bytes=256)
        nc.gpsimd.memset(brow[:], 0.0)
        nc.scalar.dma_start(out=brow[0:NBANK, :], in_=bias.rearrange("(b c) one -> b (c one)", b=NBANK))

        ident_bf = keep.tile([P, P], BF16, name="ident_bf", align_bytes=256)
        make_identity(nc, ident_bf[:])
        ident = keep.tile([P, P], F32, name="ident", align_bytes=256)
        make_identity(nc, ident[:])

        w_at = {}

        def load_words(g, first_bank, n_banks):
            cols = BANK * n_banks
            wt = keep.tile([P, cols], U32, name="w%d_%d" % (g, first_bank), align_bytes=256)
            nc.sync.dma_start(
                out=wt[:].bitcast(I32),
                in_=weight_words[g, :, BANK * first_bank : BANK * first_bank + cols, :]
                .rearrange("p n t -> p (n t)")
                .bitcast(I32),
            )
            for b in range(n_banks):
                w_at[g, first_bank + b] = (wt, BANK * b)

        def load_scales(plane, first):
            for quad in range(4):
                nc.gpsimd.dma_start(
                    out=plane[32 * quad : 32 * quad + 16, :].bitcast(F32),
                    in_=weight_scales[first : first + 4, 4 * quad : 4 * quad + 4, :].bitcast(F32),
                )

        load_scales(plane_a, 0)
        load_scales(plane_b, 4)
        for quad in range(4):
            nc.gpsimd.dma_start(
                out=plane_c[32 * quad : 32 * quad + 16, :].bitcast(F32),
                in_=weight_scales[8, 4 * quad : 4 * quad + 4, :]
                .rearrange("r (k c) -> k r c", k=4)
                .bitcast(F32),
            )
        for g in range(G_FULL):
            load_words(g, 0, NBANK)
        for first_bank, n_banks in ((0, 4), (4, 2)):
            for g in range(G_FULL, GROUPS):
                load_words(g, first_bank, n_banks)
        for g in range(G_FULL, GROUPS - 1):
            load_words(g, 6, 2)
        load_words(8, 6, 1)
        load_words(8, 7, 1)

        xs = keep.tile([P, 4, 9, P], BF16, name="xs", align_bytes=256)
        for s in range(9):
            i, j = divmod(s, 3)
            if s < 7:
                nc.vector.tensor_copy(
                    out=xs[:, :, s, :].rearrange("p d (n a b) -> p d n a b", n=2, a=8),
                    in_=xc[:, :, :, i : i + 8, j : j + 8].rearrange("p n d a b -> p d n a b"),
                )
            else:
                for n in range(2):
                    nc.scalar.copy(
                        out=xs[:, :, s, 64 * n : 64 * (n + 1)].rearrange("p d (a b) -> p d a b", a=8),
                        in_=xc[:, n, :, i : i + 8, j : j + 8],
                    )

        ct = keep.tile([P, 2, P, 9, 2], BF16, name="ct", align_bytes=256)
        bank_no = 0
        for f0, nf in ((0, 4), (4, 4), (8, 1)):
            for u in range(2):
                t1 = psum.tile([P, 8, P], BF16, name="t1_%d_%d" % (u, f0), tag="bank%d" % bank_no)
                bank_no += 1
                for a in range(2 * nf):
                    e = 4 * (f0 + a // 2) + 2 * u + a % 2
                    nc.tensor.transpose(t1[:, a, :], xs[:, e // 9, e % 9, :], ident_bf[:])
                dst = ct[:, u, :, f0 : f0 + nf, :].rearrange("q p f l -> q p (f l)")
                src = t1[:, 0 : 2 * nf, :].rearrange("q a p -> q p a")
                if u == 0:
                    nc.vector.tensor_copy(out=dst, in_=src)
                else:
                    nc.scalar.copy(out=dst, in_=src)

        cth = ct[:].rearrange("q u p f l -> q u (p f l)").bitcast(F32)
        grouped = keep.tile([P, GROUPS, 4 * P], BF16, name="grouped", align_bytes=256)
        codes = keep.tile([P, GROUPS, P], U32, name="codes", align_bytes=256)
        cplane = keep.tile([P, GROUPS, P], U8, name="cplane", align_bytes=256)
        for m in range(5):
            g0 = 2 * m
            ng = min(2, GROUPS - g0)
            t2 = psum.tile([P, 2, 2, P], F32, name="t2_%d" % m, tag="bank%d" % ((7 + m) % 8))
            for gl in range(ng):
                for u in range(2):
                    nc.tensor.transpose(
                        t2[:, gl, u, :], cth[:, u, P * (g0 + gl) : P * (g0 + gl + 1)], ident[:]
                    )
            dst = grouped[:, g0 : g0 + ng, :].bitcast(F32).rearrange("p g (q u) -> p g q u", u=2)
            src = t2[:, 0:ng].rearrange("p g u q -> p g q u")
            if m % 2 == 0:
                nc.vector.tensor_copy(out=dst, in_=src)
            else:
                nc.scalar.copy(out=dst, in_=src)
            nc.vector.quantize_mx(
                out=codes[:, g0 : g0 + ng, :].rearrange("p g q -> p (g q)").bitcast(FP8X4),
                scales=cplane[:, g0 : g0 + ng, :].rearrange("p g q -> p (g q)"),
                in_=grouped[:, g0 : g0 + ng, :].rearrange("p g c -> p (g c)"),
            )

        bsort = keep.tile([P, 4, P], F32, name="bsort", align_bytes=256)
        nc.scalar.copy(out=bsort[:], in_=brow[:].rearrange("r (j c) -> r c j", c=4))
        tb = psum.tile([P, 4, P], F32, name="tb", tag="bank4")
        for c in range(4):
            nc.tensor.transpose(tb[:, c, :], bsort[:, c, :], ident[:])
        bias_t = keep.tile([P, NBANK, 4], F32, name="bias_t", align_bytes=256)
        nc.vector.tensor_copy(out=bias_t[:], in_=tb[:, :, 0:NBANK].rearrange("j c b -> j b c"))

        def w_scale(g, b):
            if g < 4:
                return plane_a[4 * g : P, BANK * b : BANK * (b + 1)]
            if g < 8:
                return plane_b[4 * (g - 4) : P, BANK * b : BANK * (b + 1)]
            return plane_c[4 * (b // 2) : P, BANK * (b % 2) : BANK * (b % 2 + 1)]

        def mx_pass(acc, g, b):
            wt, c0 = w_at[g, b]
            rhs = wt[:, c0 : c0 + BANK]
            nc.tensor.matmul_mx(
                out=acc[:],
                lhsT=codes[:, g, :].bitcast(FP8X4),
                lhsT_scale=cplane[:, g, :],
                rhs=rhs.bitcast(FP8X4),
                rhs_scale=w_scale(g, b),
                start=(g == 0),
                stop=(g == GROUPS - 1),
            )

        accs = []
        for b in range(NBANK):
            acc = psum.tile([P, BANK], F32, name="acc%d" % b, tag="bank%d" % b)
            accs.append(acc)
        for g in range(G_FULL):
            for b in range(NBANK):
                mx_pass(accs[b], g, b)

        s_tiles = {}

        def drain_bank(b):
            s_sb = work.tile([P, 4, P], F32, name="s_sb", align_bytes=256)
            nc.scalar.copy(out=s_sb[:], in_=accs[b][:].rearrange("q (j c) -> q c j", c=4))
            s_tiles[b] = s_sb

        def finish_bank(b):
            t3 = psum.tile([P, 4, P], F32, name="t3_%d" % b, tag="bank%d" % b)
            for c in range(4):
                nc.tensor.transpose(t3[:, c, :], s_tiles[b][:, c, :], ident[:])
            o_sb = work.tile([P, 2, 4, 64], F32, name="o_sb", align_bytes=256)
            nc.vector.tensor_tensor(
                out=o_sb[:].rearrange("j n c q -> j c n q"),
                in0=t3[:].rearrange("j c (n q) -> j c n q", n=2),
                in1=bias_t[:, b, :].unsqueeze(2).unsqueeze(3).to_broadcast([P, 4, 2, 64]),
                op=mybir.AluOpType.add,
            )
            nc.sync.dma_start(
                out=out[:, BANK * b : BANK * (b + 1)].rearrange("n (j c) p q -> j n (c p q)", c=4),
                in_=o_sb[:].rearrange("j n c q -> j n (c q)"),
            )

        def passes(g, banks):
            for b in banks:
                mx_pass(accs[b], g, b)
                if g == GROUPS - 1:
                    drain_bank(b)

        for g in range(G_FULL, GROUPS):
            passes(g, (0, 1, 2, 3))
        passes(4, (4, 5))
        finish_bank(0)
        finish_bank(1)
        passes(5, (4, 5))
        finish_bank(2)
        finish_bank(3)
        for g in (6, 7, 8):
            passes(g, (4, 5))
        passes(4, (6, 7))
        finish_bank(4)
        finish_bank(5)
        for g in (5, 6, 7, 8):
            passes(g, (6, 7))
        finish_bank(6)
        finish_bank(7)
